import numpy as np
import ml_dtypes


def mxq(x, axis, fmt="e4m3"):
    dtype, down = {"e4m3": (ml_dtypes.float8_e4m3fn, 7), "e5m2": (ml_dtypes.float8_e5m2, 14)}[fmt]
    v = np.moveaxis(np.asarray(x, np.float32).astype(ml_dtypes.bfloat16).astype(np.float64), axis, -1)
    blocks = v.reshape(v.shape[:-1] + (-1, 32))
    amax = np.abs(blocks).max(-1, keepdims=True)
    byte = np.maximum(np.where(amax > 0, np.frexp(amax)[1] - 1 + 127, 0) - down, 1)
    scale = np.exp2(byte - 127.0)
    codes = (blocks / scale).astype(np.float32).astype(dtype).astype(np.float64)
    return np.moveaxis((codes * scale).reshape(v.shape), -1, axis)


WIDE = False


def mx_kscale(k):
    if not WIDE:
        return np.ones(k)
    levels = np.array([10, -10, 5, -5, 0])
    a = np.random.permutation(np.resize(levels, k // 512 * 4)).reshape(k // 512, 4)
    idx = np.arange(k)
    return np.exp2(a[idx // 512, idx % 128 // 32])


BF16 = ml_dtypes.bfloat16


def bf(x):
    return np.asarray(x, np.float32).astype(BF16)


def f64(x):
    return np.asarray(x).astype(np.float64)


B, C, H, W, ATT_DEPTH, PATCH = 1, 4, 512, 1024, 2, 8
DS = 2 ** ATT_DEPTH
HS, WS = H // (PATCH * DS), W // (PATCH * DS)
HT, WT = H // PATCH, W // PATCH
LP, L, N = HS * WS, HT * WT, C * PATCH * PATCH


def setup_inputs():
    s = mx_kscale(LP)
    sx = np.repeat(np.repeat(s.reshape(HS, WS), PATCH * DS, axis=0), PATCH * DS, axis=1)
    x = np.random.standard_normal((B, C, H, W)) * 2.0 * DS / sx
    keep = 0.25 + 0.75 * np.random.random((B, 1, L, 1))
    keep = keep * (np.random.random((B, 1, L, 1)) >= 0.03)
    a = np.random.random((B, 1, L, LP)) * (np.random.random((B, 1, L, LP)) < keep)
    return {"x": bf(x), "attentions": bf(a * 0.3 * np.sqrt(LP) * s)}


def reference(x, attentions):
    x, attentions = f64(x), f64(attentions)
    argx = x.reshape(B, C, H // DS, DS, W // DS, DS).mean(axis=(3, 5))
    unf = argx.reshape(B, C, HS, PATCH, WS, PATCH).transpose(0, 1, 3, 5, 2, 4).reshape(B, N, LP)
    nz = np.where(attentions != 0.0, 1.0, 0.0).sum(axis=-1, keepdims=True) + 1e-05
    a = attentions / nz
    att = mxq(a, 3, "e4m3") @ mxq(unf[:, None].transpose(0, 1, 3, 2), 2, "e4m3")
    att = att[:, 0].transpose(0, 2, 1)
    return att.reshape(B, C, PATCH, PATCH, HT, WT).transpose(0, 1, 4, 2, 5, 3).reshape(B, C, H, W)

@@ -1,0 +1,183 @@
+from contextlib import ExitStack
+
+import concourse.mybir as mybir
+from concourse.masks import make_identity
+
+FLOPS = 2 * 8192 * 512 * 256
+
+BF16 = mybir.dt.bfloat16
+F32 = mybir.dt.float32
+U32 = mybir.dt.uint32
+U8 = mybir.dt.uint8
+FP8X4 = mybir.dt.float8_e4m3fn_x4
+ALU = mybir.AluOpType
+AX = mybir.AxisListType
+P = 128
+CH = 8
+GRP = 16
+
+
+def tile_decode_atten_kernel(tc, x, attentions, out):
+    nc = tc.nc
+    xv = x[0].rearrange("c (hp dh) w -> hp c (dh w)", dh=4)
+    av = attentions[0, 0].rearrange("(m s) j -> m s j", s=64)
+    ov = out[0].rearrange("c (lh kh) w -> c lh kh w", kh=8)
+
+    with ExitStack() as ctx:
+        keep = ctx.enter_context(tc.tile_pool(name="keep", bufs=1))
+        work = ctx.enter_context(tc.tile_pool(name="work", bufs=2))
+        psum = ctx.enter_context(tc.psum_pool(name="psum", bufs=4))
+
+        att = []
+        xs = []
+        for k in range(8):
+            att_k = keep.tile([P, CH, 512], BF16, name="att%d" % k)
+            att.append(att_k)
+        for c in range(4):
+            xs_c = keep.tile([P, 4096], BF16, name="xs%d" % c)
+            xs.append(xs_c)
+        nc.sync.dma_start(out=att[0][:], in_=av[:, 0:CH, :])
+        for c in range(4):
+            nc.sync.dma_start(out=xs[c][:], in_=xv[:, c, :])
+        for k in range(1, 8):
+            nc.sync.dma_start(out=att[k][:], in_=av[:, k * CH : (k + 1) * CH, :])
+
+        ident = keep.tile([P, P], BF16, name="ident")
+        make_identity(nc, ident[:])
+        perm = keep.tile([P, P], BF16, name="perm")
+        nc.vector.tensor_scalar(
+            out=perm[:].rearrange("k (a t h) -> k a t h", a=4, t=4),
+            in0=ident[:].rearrange("k (t a h) -> k a t h", t=4, a=4),
+            scalar1=1.0 / 16.0,
+            scalar2=None,
+            op0=ALU.mult,
+        )
+
+        a_codes = keep.tile([P, 8192], U32, name="a_codes", align_bytes=64)
+        a_scales = keep.tile([P, 8192], U8, name="a_scales", align_bytes=64)
+        u_codes = keep.tile([P, 256], U32, name="u_codes", align_bytes=64)
+        u_scales = keep.tile([P, 256], U8, name="u_scales", align_bytes=64)
+
+        def front(k):
+            cnt = work.tile([P, CH], F32, name="cnt")
+            for i in range(CH):
+                junk = work.tile([P, 512], BF16, name="junk")
+                nc.vector.tensor_scalar(
+                    out=junk[:],
+                    in0=att[k][:, i, :],
+                    scalar1=0.0,
+                    scalar2=None,
+                    op0=ALU.not_equal,
+                    op1=ALU.add,
+                    accum_out=cnt[:, i : i + 1],
+                )
+            nz = work.tile([P, CH], F32, name="nz")
+            nc.vector.tensor_scalar_add(out=nz[:], in0=cnt[:], scalar1=1e-05)
+            rnz = work.tile([P, CH], F32, name="rnz")
+            nc.vector.reciprocal(out=rnz[:], in_=nz[:])
+            a_sb = work.tile([P, CH, 512], BF16, name="a_sb")
+            for i in range(CH):
+                nc.vector.tensor_scalar(
+                    out=a_sb[:, i, :],
+                    in0=att[k][:, i, :],
+                    scalar1=rnz[:, i : i + 1],
+                    scalar2=None,
+                    op0=ALU.mult,
+                )
+            grouped = work.tile([P, CH * 512], BF16, name="grouped", align_bytes=64)
+            for q in range(CH // 2):
+                p_t = psum.tile([P, 2, 4, P], BF16, name="p_t")
+                for i2 in range(2):
+                    for t in range(4):
+                        nc.tensor.transpose(
+                            out=p_t[:, i2, t, :],
+                            in_=a_sb[:, 2 * q + i2, t * P : (t + 1) * P],
+                            identity=ident[:],
+                        )
+                nc.scalar.copy(
+                    out=grouped[:, q * 1024 : (q + 1) * 1024].rearrange(
+                        "p (i m t) -> p i m t", i=2, t=4
+                    ),
+                    in_=p_t[:].rearrange("p i t m -> p i m t"),
+                )
+            for hq in range(2):
+                cols = slice(k * 1024 + hq * 512, k * 1024 + (hq + 1) * 512)
+                nc.vector.quantize_mx(
+                    out=a_codes[:, cols].bitcast(FP8X4),
+                    scales=a_scales[:, cols],
+                    in_=grouped[:, hq * 2048 : (hq + 1) * 2048],
+                )
+
+        def u_path():
+            g = keep.tile([P, 4, 256], BF16, name="g")
+            with nc.allow_low_precision(reason="the float32 sum of 16 pixels is rounded once to bfloat16"):
+                for c in range(4):
+                    nc.vector.tensor_reduce(
+                        out=g[:, c, :],
+                        in_=xs[c][:].rearrange("p (dh wp dw) -> p wp dh dw", dh=4, dw=4),
+                        axis=AX.XY,
+                        op=ALU.add,
+                    )
+            g3 = keep.tile([P, 1024], F32, name="g3", align_bytes=64)
+            for b in range(2):
+                g2 = psum.tile([P, 512], F32, name="acc")
+                for c2 in range(2):
+                    nc.tensor.matmul(
+                        out=g2[:, c2 * 256 : (c2 + 1) * 256].rearrange("p (kw jw) -> p kw jw", kw=8),
+                        lhsT=perm[:],
+                        rhs=g[:, 2 * b + c2, :].rearrange("p (jw kw) -> p kw jw", kw=8),
+                        start=True,
+                        stop=True,
+                    )
+                nc.vector.transpose(out=g3[:, b * 512 : (b + 1) * 512], in_=g2[:])
+            gu = keep.tile([P, 1024], BF16, name="gu", align_bytes=64)
+            for c in range(4):
+                nc.scalar.copy(
+                    out=gu[:, c * 256 : (c + 1) * 256].rearrange("p (kh kw t) -> p kh kw t", kh=8, kw=8),
+                    in_=g3[:, c * 256 : (c + 1) * 256].rearrange("p (kw t kh) -> p kh kw t", kw=8, t=4),
+                )
+            nc.vector.quantize_mx(out=u_codes[:].bitcast(FP8X4), scales=u_scales[:], in_=gu[:])
+
+        stage = {}
+
+        def back(k):
+            if (k * CH) % GRP == 0:
+                f_new = work.tile([P, 32, GRP, 8], F32, name="f_out")
+                stage["f"] = f_new
+            f_out = stage["f"]
+            for q in range(CH // 2):
+                acc = psum.tile([P, 512], F32, name="acc")
+                for i2 in range(2):
+                    s = k * CH + 2 * q + i2
+                    nc.tensor.matmul_mx(
+                        out=acc[:, i2 * 256 : (i2 + 1) * 256],
+                        lhsT=a_codes[:, s * P : (s + 1) * P].bitcast(FP8X4),
+                        lhsT_scale=a_scales[:, s * P : (s + 1) * P],
+                        rhs=u_codes[:].bitcast(FP8X4),
+                        rhs_scale=u_scales[:],
+                        start=True,
+                        stop=True,
+                    )
+                sl = (k * CH + 2 * q) % GRP
+                nc.scalar.copy(
+                    out=f_out[:, :, sl : sl + 2, :],
+                    in_=acc[:].rearrange("p (i q k) -> p q i k", i=2, k=8),
+                )
+            if ((k + 1) * CH) % GRP == 0:
+                grp = (k * CH) // GRP
+                for hf in range(2):
+                    for c in range(4):
+                        w0 = hf * 512 + grp * GRP * 8
+                        nc.sync.dma_start(
+                            out=ov[c, :, :, w0 : w0 + GRP * 8],
+                            in_=f_out[hf:P:2, c * 8 : (c + 1) * 8, :, :].rearrange("m kh s kw -> m kh (s kw)"),
+                        )
+
+        front(0)
+        u_path()
+        front(1)
+        back(0)
+        for k in range(2, 8):
+            front(k)
+            back(k - 1)
+        back(7)

@@ -13,171 +13,295 @@ FP8X4 = mybir.dt.float8_e4m3fn_x4
 ALU = mybir.AluOpType
 AX = mybir.AxisListType
 P = 128
-CH = 8
-GRP = 16
+QT = 4
+NQ = 16
+RING = 8
+GROUPS = ((0, 1, 2, 3), (4, 5, 6, 7), (8, 9, 10, 11), (12, 13), (14,), (15,))
+LEAD = 2
+OE_V = (3, 7, 11, 15, 19, 23, 27, 31)
+EV_V = ()
+FIRST_LOADS = (("a", 0), ("a", 1), ("x", 0), ("a", 2), ("x", 1), ("a", 3), ("x", 2), ("a", 4), ("x", 3), ("a", 5), ("a", 6), ("a", 7))
 
 
 def tile_decode_atten_kernel(tc, x, attentions, out):
     nc = tc.nc
-    xv = x[0].rearrange("c (hp dh) w -> hp c (dh w)", dh=4)
+    xv = x[0].rearrange("c (t q) w -> q c t w", q=P)
     av = attentions[0, 0].rearrange("(m s) j -> m s j", s=64)
     ov = out[0].rearrange("c (lh kh) w -> c lh kh w", kh=8)
 
     with ExitStack() as ctx:
         keep = ctx.enter_context(tc.tile_pool(name="keep", bufs=1))
-        work = ctx.enter_context(tc.tile_pool(name="work", bufs=2))
+        attp = ctx.enter_context(tc.tile_pool(name="attp", bufs=RING))
+        small = ctx.enter_context(tc.tile_pool(name="small", bufs=3))
+        work = ctx.enter_context(tc.tile_pool(name="work", bufs=4))
+        outp = ctx.enter_context(tc.tile_pool(name="outp", bufs=3))
         psum = ctx.enter_context(tc.psum_pool(name="psum", bufs=4))
+        ctx.enter_context(tc.manual_schedule())
 
-        att = []
-        xs = []
-        for k in range(8):
-            att_k = keep.tile([P, CH, 512], BF16, name="att%d" % k)
-            att.append(att_k)
-        for c in range(4):
-            xs_c = keep.tile([P, 4096], BF16, name="xs%d" % c)
-            xs.append(xs_c)
-        nc.sync.dma_start(out=att[0][:], in_=av[:, 0:CH, :])
-        for c in range(4):
-            nc.sync.dma_start(out=xs[c][:], in_=xv[:, c, :])
-        for k in range(1, 8):
-            nc.sync.dma_start(out=att[k][:], in_=av[:, k * CH : (k + 1) * CH, :])
+        att = {}
+        xs = {}
+        a_sb = {}
+        grouped = {}
+        p_t = {}
+        acc = {}
+        f_out = {}
+        o1 = {}
+        o1sb = {}
+        g2 = {}
+
+        def load_att(q):
+            att_q = attp.tile([P, QT, 512], BF16, name="att")
+            att[q] = att_q
+            nc.sync.dma_start(out=att_q[:], in_=av[:, q * QT : (q + 1) * QT, :])
+
+        def load_x(c):
+            xs_c = keep.tile([P, 4, 1024], BF16, name="xs%d" % c)
+            xs[c] = xs_c
+            nc.sync.dma_start(out=xs_c[:], in_=xv[:, c, :, :])
+
+        for kind, idx in FIRST_LOADS:
+            if kind == "a":
+                load_att(idx)
+            else:
+                load_x(idx)
 
         ident = keep.tile([P, P], BF16, name="ident")
         make_identity(nc, ident[:])
-        perm = keep.tile([P, P], BF16, name="perm")
-        nc.vector.tensor_scalar(
-            out=perm[:].rearrange("k (a t h) -> k a t h", a=4, t=4),
-            in0=ident[:].rearrange("k (t a h) -> k a t h", t=4, a=4),
-            scalar1=1.0 / 16.0,
-            scalar2=None,
-            op0=ALU.mult,
+        pool4 = keep.tile([P, 32], F32, name="pool4")
+        nc.vector.tensor_reduce(
+            out=pool4[:], in_=ident[:].rearrange("k (n d) -> k n d", d=4), axis=AX.X, op=ALU.add
         )
+        pool16 = keep.tile([P, 32], BF16, name="pool16")
+        nc.vector.tensor_scalar(out=pool16[:], in0=pool4[:], scalar1=1.0 / 16.0, scalar2=None, op0=ALU.mult)
 
         a_codes = keep.tile([P, 8192], U32, name="a_codes", align_bytes=64)
         a_scales = keep.tile([P, 8192], U8, name="a_scales", align_bytes=64)
         u_codes = keep.tile([P, 256], U32, name="u_codes", align_bytes=64)
         u_scales = keep.tile([P, 256], U8, name="u_scales", align_bytes=64)
+        g3 = keep.tile([P, 1024], F32, name="g3", align_bytes=64)
+        gu = keep.tile([P, 1024], BF16, name="gu", align_bytes=64)
 
-        def front(k):
-            cnt = work.tile([P, CH], F32, name="cnt")
-            for i in range(CH):
-                junk = work.tile([P, 512], BF16, name="junk")
+        def copy_on(eng, dst, src):
+            if eng == "V":
+                nc.vector.tensor_copy(out=dst, in_=src)
+            else:
+                nc.scalar.copy(out=dst, in_=src)
+
+        def front(q):
+            cnt = small.tile([P, QT], F32, name="cnt")
+            for i in range(QT):
+                junk = small.tile([P, 512], BF16, name="junk")
                 nc.vector.tensor_scalar(
                     out=junk[:],
-                    in0=att[k][:, i, :],
+                    in0=att[q][:, i, :],
                     scalar1=0.0,
                     scalar2=None,
                     op0=ALU.not_equal,
                     op1=ALU.add,
                     accum_out=cnt[:, i : i + 1],
                 )
-            nz = work.tile([P, CH], F32, name="nz")
+            nz = small.tile([P, QT], F32, name="nz")
             nc.vector.tensor_scalar_add(out=nz[:], in0=cnt[:], scalar1=1e-05)
-            rnz = work.tile([P, CH], F32, name="rnz")
+            rnz = small.tile([P, QT], F32, name="rnz")
             nc.vector.reciprocal(out=rnz[:], in_=nz[:])
-            a_sb = work.tile([P, CH, 512], BF16, name="a_sb")
-            for i in range(CH):
+            a_q = work.tile([P, QT, 512], BF16, name="a_sb")
+            a_sb[q] = a_q
+            for i in range(QT):
                 nc.vector.tensor_scalar(
-                    out=a_sb[:, i, :],
-                    in0=att[k][:, i, :],
+                    out=a_q[:, i, :],
+                    in0=att[q][:, i, :],
                     scalar1=rnz[:, i : i + 1],
                     scalar2=None,
                     op0=ALU.mult,
                 )
-            grouped = work.tile([P, CH * 512], BF16, name="grouped", align_bytes=64)
-            for q in range(CH // 2):
-                p_t = psum.tile([P, 2, 4, P], BF16, name="p_t")
-                for i2 in range(2):
-                    for t in range(4):
-                        nc.tensor.transpose(
-                            out=p_t[:, i2, t, :],
-                            in_=a_sb[:, 2 * q + i2, t * P : (t + 1) * P],
-                            identity=ident[:],
-                        )
-                nc.scalar.copy(
-                    out=grouped[:, q * 1024 : (q + 1) * 1024].rearrange(
-                        "p (i m t) -> p i m t", i=2, t=4
-                    ),
-                    in_=p_t[:].rearrange("p i t m -> p i m t"),
-                )
-            for hq in range(2):
-                cols = slice(k * 1024 + hq * 512, k * 1024 + (hq + 1) * 512)
-                nc.vector.quantize_mx(
-                    out=a_codes[:, cols].bitcast(FP8X4),
-                    scales=a_scales[:, cols],
-                    in_=grouped[:, hq * 2048 : (hq + 1) * 2048],
+
+        def tr(pr):
+            q, h = pr // 2, pr % 2
+            p_new = psum.tile([P, 2, 4, P], BF16, name="p_t")
+            p_t[pr] = p_new
+            for i2 in range(2):
+                for t in range(4):
+                    nc.tensor.transpose(
+                        out=p_new[:, i2, t, :],
+                        in_=a_sb[q][:, 2 * h + i2, t * P : (t + 1) * P],
+                        identity=ident[:],
+                    )
+
+        def ev(pr):
+            q, h = pr // 2, pr % 2
+            if h == 0:
+                g_new = work.tile([P, QT * 512], BF16, name="grouped", align_bytes=64)
+                grouped[q] = g_new
+            copy_on(
+                "V" if pr in EV_V else "S",
+                grouped[q][:, h * 1024 : (h + 1) * 1024].rearrange("p (i m t) -> p i m t", i=2, t=4),
+                p_t[pr][:].rearrange("p i t m -> p i m t"),
+            )
+
+        def qz(q):
+            cols = slice(q * 512, (q + 1) * 512)
+            nc.vector.quantize_mx(
+                out=a_codes[:, cols].bitcast(FP8X4), scales=a_scales[:, cols], in_=grouped[q][:]
+            )
+
+        def mm(pr):
+            acc_new = psum.tile([P, 512], F32, name="acc")
+            acc[pr] = acc_new
+            for i2 in range(2):
+                s = 2 * pr + i2
+                nc.tensor.matmul_mx(
+                    out=acc_new[:, i2 * 256 : (i2 + 1) * 256],
+                    lhsT=a_codes[:, s * P : (s + 1) * P].bitcast(FP8X4),
+                    lhsT_scale=a_scales[:, s * P : (s + 1) * P],
+                    rhs=u_codes[:].bitcast(FP8X4),
+                    rhs_scale=u_scales[:],
+                    start=True,
+                    stop=True,
                 )
 
-        def u_path():
-            g = keep.tile([P, 4, 256], BF16, name="g")
-            with nc.allow_low_precision(reason="the float32 sum of 16 pixels is rounded once to bfloat16"):
+        def group_of(q):
+            for g, members in enumerate(GROUPS):
+                if q in members:
+                    return g
+            return -1
+
+        def oe(pr, eng):
+            g = group_of(pr // 2)
+            width = len(GROUPS[g]) * QT
+            if g not in f_out:
+                f_new = outp.tile([P, 32, width, 8], F32, name="f_out")
+                f_out[g] = f_new
+            sl = 2 * pr - GROUPS[g][0] * QT
+            copy_on(
+                eng,
+                f_out[g][:, :, sl : sl + 2, :],
+                acc[pr][:].rearrange("p (i q k) -> p q i k", i=2, k=8),
+            )
+
+        def st(g):
+            width = len(GROUPS[g]) * QT * 8
+            for hf in range(2):
                 for c in range(4):
-                    nc.vector.tensor_reduce(
-                        out=g[:, c, :],
-                        in_=xs[c][:].rearrange("p (dh wp dw) -> p wp dh dw", dh=4, dw=4),
-                        axis=AX.XY,
-                        op=ALU.add,
+                    w0 = hf * 512 + GROUPS[g][0] * QT * 8
+                    nc.sync.dma_start(
+                        out=ov[c, :, :, w0 : w0 + width],
+                        in_=f_out[g][hf:P:2, c * 8 : (c + 1) * 8, :, :].rearrange("m kh s kw -> m kh (s kw)"),
                     )
-            g3 = keep.tile([P, 1024], F32, name="g3", align_bytes=64)
-            for b in range(2):
-                g2 = psum.tile([P, 512], F32, name="acc")
-                for c2 in range(2):
-                    nc.tensor.matmul(
-                        out=g2[:, c2 * 256 : (c2 + 1) * 256].rearrange("p (kw jw) -> p kw jw", kw=8),
-                        lhsT=perm[:],
-                        rhs=g[:, 2 * b + c2, :].rearrange("p (jw kw) -> p kw jw", kw=8),
-                        start=True,
-                        stop=True,
-                    )
-                nc.vector.transpose(out=g3[:, b * 512 : (b + 1) * 512], in_=g2[:])
-            gu = keep.tile([P, 1024], BF16, name="gu", align_bytes=64)
-            for c in range(4):
+
+        def s1(c):
+            for h in range(2):
+                o_new = psum.tile([P, 4, 4, 4, 8], F32, name="acc")
+                o1[(c, h)] = o_new
+                for jl in range(4):
+                    for t in range(4):
+                        jq = 4 * h + jl
+                        nc.tensor.matmul(
+                            out=o_new[:, jl, :, t, :],
+                            lhsT=xs[c][:, t, jq * P : (jq + 1) * P],
+                            rhs=pool16[:].rearrange("q (a k) -> q a k", a=4),
+                            start=True,
+                            stop=True,
+                        )
+
+        def xe(c):
+            o_sb = work.tile([P, 1024], F32, name="o1sb")
+            o1sb[c] = o_sb
+            for h in range(2):
+                nc.scalar.copy(
+                    out=o_sb[:, h * 512 : (h + 1) * 512],
+                    in_=o1[(c, h)][:].rearrange("p j a t k -> p (j a t k)"),
+                )
+
+        def s2(c):
+            b, c2 = c // 2, c % 2
+            if c2 == 0:
+                g_new = psum.tile([P, 2, 8, 8, 4], F32, name="acc")
+                g2[b] = g_new
+            for jq in range(8):
+                nc.tensor.matmul(
+                    out=g2[b][:, c2, :, jq, :].rearrange("p kw j4 -> p j4 kw"),
+                    lhsT=o1sb[c][:, jq * P : (jq + 1) * P],
+                    rhs=pool4[:].rearrange("r (j4 kw) -> r j4 kw", j4=4),
+                    start=True,
+                    stop=True,
+                )
+
+        def vt(b):
+            nc.vector.transpose(
+                out=g3[:, b * 512 : (b + 1) * 512], in_=g2[b][:].rearrange("p c kw jq j4 -> p (c kw jq j4)")
+            )
+
+        def gucopy(b):
+            for c in (2 * b, 2 * b + 1):
                 nc.scalar.copy(
                     out=gu[:, c * 256 : (c + 1) * 256].rearrange("p (kh kw t) -> p kh kw t", kh=8, kw=8),
                     in_=g3[:, c * 256 : (c + 1) * 256].rearrange("p (kw t kh) -> p kh kw t", kw=8, t=4),
                 )
+
+        def qu():
             nc.vector.quantize_mx(out=u_codes[:].bitcast(FP8X4), scales=u_scales[:], in_=gu[:])
 
-        stage = {}
+        state = {"front": 0, "qz": 0, "mm": 0, "st": 0, "load": RING}
+        done = set()
+        pend_v = []
 
-        def back(k):
-            if (k * CH) % GRP == 0:
-                f_new = work.tile([P, 32, GRP, 8], F32, name="f_out")
-                stage["f"] = f_new
-            f_out = stage["f"]
-            for q in range(CH // 2):
-                acc = psum.tile([P, 512], F32, name="acc")
-                for i2 in range(2):
-                    s = k * CH + 2 * q + i2
-                    nc.tensor.matmul_mx(
-                        out=acc[:, i2 * 256 : (i2 + 1) * 256],
-                        lhsT=a_codes[:, s * P : (s + 1) * P].bitcast(FP8X4),
-                        lhsT_scale=a_scales[:, s * P : (s + 1) * P],
-                        rhs=u_codes[:].bitcast(FP8X4),
-                        rhs_scale=u_scales[:],
-                        start=True,
-                        stop=True,
-                    )
-                sl = (k * CH + 2 * q) % GRP
-                nc.scalar.copy(
-                    out=f_out[:, :, sl : sl + 2, :],
-                    in_=acc[:].rearrange("p (i q k) -> p q i k", i=2, k=8),
-                )
-            if ((k + 1) * CH) % GRP == 0:
-                grp = (k * CH) // GRP
-                for hf in range(2):
-                    for c in range(4):
-                        w0 = hf * 512 + grp * GRP * 8
-                        nc.sync.dma_start(
-                            out=ov[c, :, :, w0 : w0 + GRP * 8],
-                            in_=f_out[hf:P:2, c * 8 : (c + 1) * 8, :, :].rearrange("m kh s kw -> m kh (s kw)"),
-                        )
+        def next_front():
+            q = state["front"]
+            if q < NQ:
+                front(q)
+                state["front"] = q + 1
+                if state["load"] < NQ:
+                    load_att(state["load"])
+                    state["load"] = state["load"] + 1
 
-        front(0)
-        u_path()
-        front(1)
-        back(0)
-        for k in range(2, 8):
-            front(k)
-            back(k - 1)
-        back(7)
+        def flush_stores():
+            while state["st"] < len(GROUPS) and all(
+                (2 * q in done) and (2 * q + 1 in done) for q in GROUPS[state["st"]]
+            ):
+                st(state["st"])
+                state["st"] = state["st"] + 1
+
+        for k in range(LEAD):
+            next_front()
+        for i in range(NQ + 10):
+            for pr in pend_v:
+                oe(pr, "V")
+                done.add(pr)
+            pend_v = []
+            flush_stores()
+            if i < NQ:
+                tr(2 * i)
+                tr(2 * i + 1)
+                ev(2 * i)
+                ev(2 * i + 1)
+            next_front()
+            if i < 4:
+                s1(i)
+                xe(i)
+            if 1 <= i <= 4:
+                s2(i - 1)
+                if i % 2 == 0:
+                    vt(i // 2 - 1)
+                    gucopy(i // 2 - 1)
+                if i == 4:
+                    qu()
+            ready = state["qz"]
+            if i >= 1 and state["qz"] < NQ:
+                qz(state["qz"])
+                state["qz"] = state["qz"] + 1
+            if i >= 4:
+                todo = []
+                while len(todo) < 2 and state["mm"] < ready:
+                    todo.append(state["mm"])
+                    state["mm"] = state["mm"] + 1
+                for q in todo:
+                    mm(2 * q)
+                    mm(2 * q + 1)
+                for q in todo:
+                    for pr in (2 * q, 2 * q + 1):
+                        if pr in OE_V:
+                            pend_v.append(pr)
+                        else:
+                            oe(pr, "S")
+                            done.add(pr)
+                flush_stores()

@@ -20,6 +20,7 @@ GROUPS = ((0, 1, 2, 3), (4, 5, 6, 7), (8, 9, 10, 11), (12, 13), (14,), (15,))
 LEAD = 2
 OE_V = (3, 7, 11, 15, 19, 23, 27, 31)
 EV_V = ()
+N_WARM = 12
 FIRST_LOADS = (("a", 0), ("a", 1), ("x", 0), ("a", 2), ("x", 1), ("a", 3), ("x", 2), ("a", 4), ("x", 3), ("a", 5), ("a", 6), ("a", 7))
 
 
@@ -64,6 +65,27 @@ def tile_decode_atten_kernel(tc, x, attentions, out):
                 load_att(idx)
             else:
                 load_x(idx)
+
+        z_codes = keep.tile([P, 512], U32, name="z_codes", align_bytes=64)
+        z_scales = keep.tile([P, 512], U8, name="z_scales", align_bytes=64)
+        z_in = keep.tile([P, 2048], BF16, name="z_in", align_bytes=64)
+        nc.vector.memset(z_in[:], 0.0)
+        nc.vector.quantize_mx(out=z_codes[:].bitcast(FP8X4), scales=z_scales[:], in_=z_in[:])
+        warm = psum.tile([P, 512], F32, name="warm", bufs=1)
+
+        def dummy(n):
+            for k in range(n):
+                nc.tensor.matmul_mx(
+                    out=warm[:],
+                    lhsT=z_codes[:, 0:P].bitcast(FP8X4),
+                    lhsT_scale=z_scales[:, 0:P],
+                    rhs=z_codes[:].bitcast(FP8X4),
+                    rhs_scale=z_scales[:],
+                    start=True,
+                    stop=True,
+                )
+
+        dummy(N_WARM)
 
         ident = keep.tile([P, P], BF16, name="ident")
         make_identity(nc, ident[:])
@@ -117,7 +139,7 @@ def tile_decode_atten_kernel(tc, x, attentions, out):
 
         def tr(pr):
             q, h = pr // 2, pr % 2
-            p_new = psum.tile([P, 2, 4, P], BF16, name="p_t")
+            p_new = psum.tile([P, 2, 4, P], BF16, name="p_t", bufs=3)
             p_t[pr] = p_new
             for i2 in range(2):
                 for t in range(4):
@@ -269,11 +291,29 @@ def tile_decode_atten_kernel(tc, x, attentions, out):
                 done.add(pr)
             pend_v = []
             flush_stores()
-            if i < NQ:
-                tr(2 * i)
-                tr(2 * i + 1)
-                ev(2 * i)
-                ev(2 * i + 1)
+            todo = []
+            if i >= 5:
+                while len(todo) < 4 and state["mm"] < 2 * state["qz"]:
+                    todo.append(state["mm"])
+                    state["mm"] = state["mm"] + 1
+            halves = (todo[: len(todo) // 2], todo[len(todo) // 2 :])
+            for h in range(2):
+                if i < NQ:
+                    tr(2 * i + h)
+                for pr in halves[h]:
+                    mm(pr)
+                if state["mm"] < 2 * NQ or halves[h]:
+                    dummy(1)
+            for h in range(2):
+                if i < NQ:
+                    ev(2 * i + h)
+                for pr in halves[h]:
+                    if pr in OE_V:
+                        pend_v.append(pr)
+                    else:
+                        oe(pr, "S")
+                        done.add(pr)
+            flush_stores()
             next_front()
             if i < 4:
                 s1(i)
@@ -285,23 +325,6 @@ def tile_decode_atten_kernel(tc, x, attentions, out):
                     gucopy(i // 2 - 1)
                 if i == 4:
                     qu()
-            ready = state["qz"]
             if i >= 1 and state["qz"] < NQ:
                 qz(state["qz"])
                 state["qz"] = state["qz"] + 1
-            if i >= 4:
-                todo = []
-                while len(todo) < 2 and state["mm"] < ready:
-                    todo.append(state["mm"])
-                    state["mm"] = state["mm"] + 1
-                for q in todo:
-                    mm(2 * q)
-                    mm(2 * q + 1)
-                for q in todo:
-                    for pr in (2 * q, 2 * q + 1):
-                        if pr in OE_V:
-                            pend_v.append(pr)
-                        else:
-                            oe(pr, "S")
-                            done.add(pr)
-                flush_stores()

@@ -17,8 +17,7 @@ QT = 4
 NQ = 16
 RING = 8
 GROUPS = ((0, 1, 2, 3), (4, 5, 6, 7), (8, 9, 10, 11), (12, 13), (14,), (15,))
-LEAD = 2
-OE_V = (3, 7, 11, 15, 19, 23, 27, 31)
+OE_V = ()
 EV_V = ()
 N_WARM = 12
 FIRST_LOADS = (("a", 0), ("a", 1), ("x", 0), ("a", 2), ("x", 1), ("a", 3), ("x", 2), ("a", 4), ("x", 3), ("a", 5), ("a", 6), ("a", 7))
@@ -109,8 +108,13 @@ def tile_decode_atten_kernel(tc, x, attentions, out):
             else:
                 nc.scalar.copy(out=dst, in_=src)
 
-        def front(q):
-            cnt = small.tile([P, QT], F32, name="cnt")
+        cnts = {}
+        nzs = {}
+        rnzs = {}
+
+        def cnt(q):
+            c_new = small.tile([P, QT], F32, name="cnt")
+            cnts[q] = c_new
             for i in range(QT):
                 junk = small.tile([P, 512], BF16, name="junk")
                 nc.vector.tensor_scalar(
@@ -120,22 +124,33 @@ def tile_decode_atten_kernel(tc, x, attentions, out):
                     scalar2=None,
                     op0=ALU.not_equal,
                     op1=ALU.add,
-                    accum_out=cnt[:, i : i + 1],
+                    accum_out=c_new[:, i : i + 1],
                 )
+
+        def fin1(q):
             nz = small.tile([P, QT], F32, name="nz")
-            nc.vector.tensor_scalar_add(out=nz[:], in0=cnt[:], scalar1=1e-05)
+            nzs[q] = nz
+            nc.vector.tensor_scalar_add(out=nz[:], in0=cnts[q][:], scalar1=1e-05)
+
+        def fin2(q):
             rnz = small.tile([P, QT], F32, name="rnz")
-            nc.vector.reciprocal(out=rnz[:], in_=nz[:])
+            rnzs[q] = rnz
+            nc.vector.reciprocal(out=rnz[:], in_=nzs[q][:])
+
+        def scl(q):
             a_q = work.tile([P, QT, 512], BF16, name="a_sb")
             a_sb[q] = a_q
             for i in range(QT):
                 nc.vector.tensor_scalar(
                     out=a_q[:, i, :],
                     in0=att[q][:, i, :],
-                    scalar1=rnz[:, i : i + 1],
+                    scalar1=rnzs[q][:, i : i + 1],
                     scalar2=None,
                     op0=ALU.mult,
                 )
+            if state["load"] < NQ:
+                load_att(state["load"])
+                state["load"] = state["load"] + 1
 
         def tr(pr):
             q, h = pr // 2, pr % 2
@@ -263,18 +278,9 @@ def tile_decode_atten_kernel(tc, x, attentions, out):
         def qu():
             nc.vector.quantize_mx(out=u_codes[:].bitcast(FP8X4), scales=u_scales[:], in_=gu[:])
 
-        state = {"front": 0, "qz": 0, "mm": 0, "st": 0, "load": RING}
+        state = {"qz": 0, "mm": 0, "st": 0, "load": RING}
         done = set()
         pend_v = []
-
-        def next_front():
-            q = state["front"]
-            if q < NQ:
-                front(q)
-                state["front"] = q + 1
-                if state["load"] < NQ:
-                    load_att(state["load"])
-                    state["load"] = state["load"] + 1
 
         def flush_stores():
             while state["st"] < len(GROUPS) and all(
@@ -283,8 +289,17 @@ def tile_decode_atten_kernel(tc, x, attentions, out):
                 st(state["st"])
                 state["st"] = state["st"] + 1
 
-        for k in range(LEAD):
-            next_front()
+        cnt(0)
+        fin1(0)
+        fin2(0)
+        scl(0)
+        cnt(1)
+        fin1(1)
+        cnt(2)
+        fin2(1)
+        scl(1)
+        fin1(2)
+        fin2(2)
         for i in range(NQ + 10):
             for pr in pend_v:
                 oe(pr, "V")
@@ -314,7 +329,12 @@ def tile_decode_atten_kernel(tc, x, attentions, out):
                         oe(pr, "S")
                         done.add(pr)
             flush_stores()
-            next_front()
+            if i + 3 < NQ:
+                cnt(i + 3)
+            if i + 2 < NQ:
+                scl(i + 2)
+            if i + 3 < NQ:
+                fin1(i + 3)
             if i < 4:
                 s1(i)
                 xe(i)
@@ -328,3 +348,5 @@ def tile_decode_atten_kernel(tc, x, attentions, out):
             if i >= 1 and state["qz"] < NQ:
                 qz(state["qz"])
                 state["qz"] = state["qz"] + 1
+            if i + 3 < NQ:
+                fin2(i + 3)

@@ -219,11 +219,14 @@ def tile_decode_atten_kernel(tc, x, attentions, out):
             width = len(GROUPS[g]) * QT * 8
             for hf in range(2):
                 for c in range(4):
-                    w0 = hf * 512 + GROUPS[g][0] * QT * 8
-                    nc.sync.dma_start(
-                        out=ov[c, :, :, w0 : w0 + width],
-                        in_=f_out[g][hf:P:2, c * 8 : (c + 1) * 8, :, :].rearrange("m kh s kw -> m kh (s kw)"),
-                    )
+                    for k2 in range(2):
+                        w0 = hf * 512 + GROUPS[g][0] * QT * 8
+                        nc.sync.dma_start(
+                            out=ov[c, :, k2 * 4 : (k2 + 1) * 4, w0 : w0 + width],
+                            in_=f_out[g][hf:P:2, c * 8 + k2 * 4 : c * 8 + (k2 + 1) * 4, :, :].rearrange(
+                                "m kh s kw -> m kh (s kw)"
+                            ),
+                        )
 
         def s1(c):
             for h in range(2):

@@ -16,8 +16,8 @@ P = 128
 QT = 4
 NQ = 16
 RING = 8
-GROUPS = ((0, 1, 2, 3), (4, 5, 6, 7), (8, 9, 10, 11), (12, 13), (14,), (15,))
-OE_V = ()
+GROUPS = ((0, 1, 2, 3), (4, 5, 6, 7), (8, 9, 10, 11), (12, 13, 14, 15))
+OE_V = (3, 7, 11, 15, 19, 23, 27)
 EV_V = ()
 N_WARM = 12
 FIRST_LOADS = (("a", 0), ("a", 1), ("x", 0), ("a", 2), ("x", 1), ("a", 3), ("x", 2), ("a", 4), ("x", 3), ("a", 5), ("a", 6), ("a", 7))
@@ -219,14 +219,11 @@ def tile_decode_atten_kernel(tc, x, attentions, out):
             width = len(GROUPS[g]) * QT * 8
             for hf in range(2):
                 for c in range(4):
-                    for k2 in range(2):
-                        w0 = hf * 512 + GROUPS[g][0] * QT * 8
-                        nc.sync.dma_start(
-                            out=ov[c, :, k2 * 4 : (k2 + 1) * 4, w0 : w0 + width],
-                            in_=f_out[g][hf:P:2, c * 8 + k2 * 4 : c * 8 + (k2 + 1) * 4, :, :].rearrange(
-                                "m kh s kw -> m kh (s kw)"
-                            ),
-                        )
+                    w0 = hf * 512 + GROUPS[g][0] * QT * 8
+                    nc.sync.dma_start(
+                        out=ov[c, :, :, w0 : w0 + width],
+                        in_=f_out[g][hf:P:2, c * 8 : (c + 1) * 8, :, :].rearrange("m kh s kw -> m kh (s kw)"),
+                    )
 
         def s1(c):
             for h in range(2):

@@ -217,13 +217,17 @@ def tile_decode_atten_kernel(tc, x, attentions, out):
 
         def st(g):
             width = len(GROUPS[g]) * QT * 8
-            for hf in range(2):
-                for c in range(4):
-                    w0 = hf * 512 + GROUPS[g][0] * QT * 8
-                    nc.sync.dma_start(
-                        out=ov[c, :, :, w0 : w0 + width],
-                        in_=f_out[g][hf:P:2, c * 8 : (c + 1) * 8, :, :].rearrange("m kh s kw -> m kh (s kw)"),
-                    )
+            for c in range(4):
+                for k2 in range(2):
+                    for hf in range(2):
+                        w0 = hf * 512 + GROUPS[g][0] * QT * 8
+                        queue = nc.sync if hf == 0 else nc.scalar
+                        queue.dma_start(
+                            out=ov[c, :, k2 * 4 : (k2 + 1) * 4, w0 : w0 + width],
+                            in_=f_out[g][hf:P:2, c * 8 + k2 * 4 : c * 8 + (k2 + 1) * 4, :, :].rearrange(
+                                "m kh s kw -> m kh (s kw)"
+                            ),
+                        )
 
         def s1(c):
             for h in range(2):

@@ -17,9 +17,9 @@ QT = 4
 NQ = 16
 RING = 8
 GROUPS = ((0, 1, 2, 3), (4, 5, 6, 7), (8, 9, 10, 11), (12, 13, 14, 15))
-OE_V = (3, 7, 11, 15, 19, 23, 27)
-EV_V = ()
-N_WARM = 12
+OE_V = (3, 7, 11, 15, 19, 23, 27, 31)
+EV_V = (31,)
+N_WARM = 6
 FIRST_LOADS = (("a", 0), ("a", 1), ("x", 0), ("a", 2), ("x", 1), ("a", 3), ("x", 2), ("a", 4), ("x", 3), ("a", 5), ("a", 6), ("a", 7))
 
 
@@ -32,7 +32,7 @@ def tile_decode_atten_kernel(tc, x, attentions, out):
     with ExitStack() as ctx:
         keep = ctx.enter_context(tc.tile_pool(name="keep", bufs=1))
         attp = ctx.enter_context(tc.tile_pool(name="attp", bufs=RING))
-        small = ctx.enter_context(tc.tile_pool(name="small", bufs=3))
+        small = ctx.enter_context(tc.tile_pool(name="small", bufs=4))
         work = ctx.enter_context(tc.tile_pool(name="work", bufs=4))
         outp = ctx.enter_context(tc.tile_pool(name="outp", bufs=3))
         psum = ctx.enter_context(tc.psum_pool(name="psum", bufs=4))
@@ -52,7 +52,11 @@ def tile_decode_atten_kernel(tc, x, attentions, out):
         def load_att(q):
             att_q = attp.tile([P, QT, 512], BF16, name="att")
             att[q] = att_q
-            nc.sync.dma_start(out=att_q[:], in_=av[:, q * QT : (q + 1) * QT, :])
+            if q == 0:
+                for h in range(2):
+                    nc.sync.dma_start(out=att_q[:, 2 * h : 2 * h + 2, :], in_=av[:, 2 * h : 2 * h + 2, :])
+            else:
+                nc.sync.dma_start(out=att_q[:], in_=av[:, q * QT : (q + 1) * QT, :])
 
         def load_x(c):
             xs_c = keep.tile([P, 4, 1024], BF16, name="xs%d" % c)
@@ -112,10 +116,10 @@ def tile_decode_atten_kernel(tc, x, attentions, out):
         nzs = {}
         rnzs = {}
 
-        def cnt(q):
+        def cnt(q, lo=0, hi=QT):
             c_new = small.tile([P, QT], F32, name="cnt")
-            cnts[q] = c_new
-            for i in range(QT):
+            cnts[(q, lo)] = c_new
+            for i in range(lo, hi):
                 junk = small.tile([P, 512], BF16, name="junk")
                 nc.vector.tensor_scalar(
                     out=junk[:],
@@ -127,28 +131,29 @@ def tile_decode_atten_kernel(tc, x, attentions, out):
                     accum_out=c_new[:, i : i + 1],
                 )
 
-        def fin1(q):
+        def fin1(q, lo=0, hi=QT):
             nz = small.tile([P, QT], F32, name="nz")
-            nzs[q] = nz
-            nc.vector.tensor_scalar_add(out=nz[:], in0=cnts[q][:], scalar1=1e-05)
+            nzs[(q, lo)] = nz
+            nc.vector.tensor_scalar_add(out=nz[:, lo:hi], in0=cnts[(q, lo)][:, lo:hi], scalar1=1e-05)
 
-        def fin2(q):
+        def fin2(q, lo=0, hi=QT):
             rnz = small.tile([P, QT], F32, name="rnz")
-            rnzs[q] = rnz
-            nc.vector.reciprocal(out=rnz[:], in_=nzs[q][:])
+            rnzs[(q, lo)] = rnz
+            nc.vector.reciprocal(out=rnz[:, lo:hi], in_=nzs[(q, lo)][:, lo:hi])
 
-        def scl(q):
-            a_q = work.tile([P, QT, 512], BF16, name="a_sb")
-            a_sb[q] = a_q
-            for i in range(QT):
+        def scl(q, lo=0, hi=QT):
+            if lo == 0:
+                a_new = work.tile([P, QT, 512], BF16, name="a_sb")
+                a_sb[q] = a_new
+            for i in range(lo, hi):
                 nc.vector.tensor_scalar(
-                    out=a_q[:, i, :],
+                    out=a_sb[q][:, i, :],
                     in0=att[q][:, i, :],
-                    scalar1=rnzs[q][:, i : i + 1],
+                    scalar1=rnzs[(q, lo)][:, i : i + 1],
                     scalar2=None,
                     op0=ALU.mult,
                 )
-            if state["load"] < NQ:
+            if hi == QT and state["load"] < NQ:
                 load_att(state["load"])
                 state["load"] = state["load"] + 1
 
@@ -217,17 +222,15 @@ def tile_decode_atten_kernel(tc, x, attentions, out):
 
         def st(g):
             width = len(GROUPS[g]) * QT * 8
+            last = g == len(GROUPS) - 1
             for c in range(4):
-                for k2 in range(2):
-                    for hf in range(2):
-                        w0 = hf * 512 + GROUPS[g][0] * QT * 8
-                        queue = nc.sync if hf == 0 else nc.scalar
-                        queue.dma_start(
-                            out=ov[c, :, k2 * 4 : (k2 + 1) * 4, w0 : w0 + width],
-                            in_=f_out[g][hf:P:2, c * 8 + k2 * 4 : c * 8 + (k2 + 1) * 4, :, :].rearrange(
-                                "m kh s kw -> m kh (s kw)"
-                            ),
-                        )
+                for hf in range(2):
+                    w0 = hf * 512 + GROUPS[g][0] * QT * 8
+                    queue = nc.scalar if (last and hf == 1) else nc.sync
+                    queue.dma_start(
+                        out=ov[c, :, :, w0 : w0 + width],
+                        in_=f_out[g][hf:P:2, c * 8 : (c + 1) * 8, :, :].rearrange("m kh s kw -> m kh (s kw)"),
+                    )
 
         def s1(c):
             for h in range(2):
@@ -274,9 +277,13 @@ def tile_decode_atten_kernel(tc, x, attentions, out):
 
         def gucopy(b):
             for c in (2 * b, 2 * b + 1):
-                nc.scalar.copy(
+                nc.gpsimd.tensor_scalar(
                     out=gu[:, c * 256 : (c + 1) * 256].rearrange("p (kh kw t) -> p kh kw t", kh=8, kw=8),
-                    in_=g3[:, c * 256 : (c + 1) * 256].rearrange("p (kw t kh) -> p kh kw t", kw=8, t=4),
+                    in0=g3[:, c * 256 : (c + 1) * 256].rearrange("p (kw t kh) -> p kh kw t", kw=8, t=4),
+                    scalar1=1.0,
+                    scalar2=0.0,
+                    op0=ALU.mult,
+                    op1=ALU.add,
                 )
 
         def qu():
@@ -293,11 +300,15 @@ def tile_decode_atten_kernel(tc, x, attentions, out):
                 st(state["st"])
                 state["st"] = state["st"] + 1
 
-        cnt(0)
-        fin1(0)
-        fin2(0)
-        scl(0)
+        cnt(0, 0, 2)
+        fin1(0, 0, 2)
+        fin2(0, 0, 2)
+        scl(0, 0, 2)
+        cnt(0, 2, 4)
+        fin1(0, 2, 4)
         cnt(1)
+        fin2(0, 2, 4)
+        scl(0, 2, 4)
         fin1(1)
         cnt(2)
         fin2(1)

@@ -17,7 +17,7 @@ QT = 4
 NQ = 16
 RING = 8
 GROUPS = ((0, 1, 2, 3), (4, 5, 6, 7), (8, 9, 10, 11), (12, 13, 14, 15))
-OE_V = (3, 7, 11, 15, 19, 23, 27, 31)
+OE_V = (29, 31)
 EV_V = (31,)
 N_WARM = 6
 FIRST_LOADS = (("a", 0), ("a", 1), ("x", 0), ("a", 2), ("x", 1), ("a", 3), ("x", 2), ("a", 4), ("x", 3), ("a", 5), ("a", 6), ("a", 7))
@@ -90,7 +90,7 @@ def tile_decode_atten_kernel(tc, x, attentions, out):
 
         dummy(N_WARM)
 
-        ident = keep.tile([P, P], BF16, name="ident")
+        ident = keep.tile([P, P], F32, name="ident")
         make_identity(nc, ident[:])
         pool4 = keep.tile([P, 32], F32, name="pool4")
         nc.vector.tensor_reduce(
@@ -159,13 +159,14 @@ def tile_decode_atten_kernel(tc, x, attentions, out):
 
         def tr(pr):
             q, h = pr // 2, pr % 2
-            p_new = psum.tile([P, 2, 4, P], BF16, name="p_t", bufs=3)
+            p_new = psum.tile([P, 2, 2, P], F32, name="p_t", bufs=3)
             p_t[pr] = p_new
             for i2 in range(2):
-                for t in range(4):
+                words = a_sb[q][:, 2 * h + i2, :].bitcast(F32)
+                for u in range(2):
                     nc.tensor.transpose(
-                        out=p_new[:, i2, t, :],
-                        in_=a_sb[q][:, 2 * h + i2, t * P : (t + 1) * P],
+                        out=p_new[:, i2, u, :],
+                        in_=words[:, u * P : (u + 1) * P],
                         identity=ident[:],
                     )
 
@@ -176,8 +177,8 @@ def tile_decode_atten_kernel(tc, x, attentions, out):
                 grouped[q] = g_new
             copy_on(
                 "V" if pr in EV_V else "S",
-                grouped[q][:, h * 1024 : (h + 1) * 1024].rearrange("p (i m t) -> p i m t", i=2, t=4),
-                p_t[pr][:].rearrange("p i t m -> p i m t"),
+                grouped[q][:, h * 1024 : (h + 1) * 1024].bitcast(F32).rearrange("p (i m u) -> p i m u", i=2, u=2),
+                p_t[pr][:].rearrange("p i u m -> p i m u"),
             )
 
         def qz(q):
@@ -234,52 +235,60 @@ def tile_decode_atten_kernel(tc, x, attentions, out):
 
         def s1(c):
             for h in range(2):
-                o_new = psum.tile([P, 4, 4, 4, 8], F32, name="acc")
+                o_new = psum.tile([P, 512], F32, name="acc")
                 o1[(c, h)] = o_new
+                o_view = o_new[:].rearrange(
+                    "p (jl alo tlo ahi thi k) -> p jl alo tlo ahi thi k", jl=4, alo=2, tlo=2, ahi=2, thi=2
+                )
                 for jl in range(4):
                     for t in range(4):
                         jq = 4 * h + jl
                         nc.tensor.matmul(
-                            out=o_new[:, jl, :, t, :],
+                            out=o_view[:, jl, :, t % 2, :, t // 2, :],
                             lhsT=xs[c][:, t, jq * P : (jq + 1) * P],
-                            rhs=pool16[:].rearrange("q (a k) -> q a k", a=4),
+                            rhs=pool16[:].rearrange("q (ahi alo k) -> q alo ahi k", ahi=2, alo=2),
                             start=True,
                             stop=True,
                         )
 
         def xe(c):
-            o_sb = work.tile([P, 1024], F32, name="o1sb")
-            o1sb[c] = o_sb
-            for h in range(2):
-                nc.scalar.copy(
-                    out=o_sb[:, h * 512 : (h + 1) * 512],
-                    in_=o1[(c, h)][:].rearrange("p j a t k -> p (j a t k)"),
-                )
-
-        def s2(c):
             b, c2 = c // 2, c % 2
             if c2 == 0:
-                g_new = psum.tile([P, 2, 8, 8, 4], F32, name="acc")
-                g2[b] = g_new
-            for jq in range(8):
-                nc.tensor.matmul(
-                    out=g2[b][:, c2, :, jq, :].rearrange("p kw j4 -> p j4 kw"),
-                    lhsT=o1sb[c][:, jq * P : (jq + 1) * P],
-                    rhs=pool4[:].rearrange("r (j4 kw) -> r j4 kw", j4=4),
-                    start=True,
-                    stop=True,
+                o_sb = keep.tile([P, 2048], F32, name="o1sb%d" % b)
+                o1sb[b] = o_sb
+            for h in range(2):
+                nc.scalar.copy(
+                    out=o1sb[b][:].rearrange("p (r c k) -> p r c k", c=2, k=8)[:, h * 64 : (h + 1) * 64, c2, :],
+                    in_=o1[(c, h)][:].rearrange("p (r k) -> p r k", k=8),
                 )
+
+        def s2(b):
+            g_new = psum.tile([P, 512], F32, name="acc")
+            g2[b] = g_new
+            g_view = g_new[:].rearrange("p (m alo jq hi) -> p alo jq m hi", m=16, alo=2, jq=8)
+            for jq in range(8):
+                for alo in range(2):
+                    nc.tensor.matmul(
+                        out=g_view[:, alo, jq, :, :],
+                        lhsT=o1sb[b][:, (2 * jq + alo) * P : (2 * jq + alo + 1) * P],
+                        rhs=pool4[:].rearrange("r (hi m) -> r m hi", hi=2),
+                        start=True,
+                        stop=True,
+                    )
 
         def vt(b):
             nc.vector.transpose(
-                out=g3[:, b * 512 : (b + 1) * 512], in_=g2[b][:].rearrange("p c kw jq j4 -> p (c kw jq j4)")
+                out=g3[:, b * 512 : (b + 1) * 512], in_=g2[b][:]
             )
 
         def gucopy(b):
-            for c in (2 * b, 2 * b + 1):
+            for c2 in range(2):
+                c = 2 * b + c2
                 nc.gpsimd.tensor_scalar(
-                    out=gu[:, c * 256 : (c + 1) * 256].rearrange("p (kh kw t) -> p kh kw t", kh=8, kw=8),
-                    in0=g3[:, c * 256 : (c + 1) * 256].rearrange("p (kw t kh) -> p kh kw t", kw=8, t=4),
+                    out=gu[:, c * 256 : (c + 1) * 256].rearrange("p (kh m lo) -> p kh m lo", kh=8, m=16),
+                    in0=g3[:, b * 512 : (b + 1) * 512].rearrange("p (lo m c kh) -> p c kh m lo", lo=2, m=16, c=2)[
+                        :, c2, :, :, :
+                    ],
                     scalar1=1.0,
                     scalar2=0.0,
                     op0=ALU.mult,
@@ -353,11 +362,10 @@ def tile_decode_atten_kernel(tc, x, attentions, out):
             if i < 4:
                 s1(i)
                 xe(i)
-            if 1 <= i <= 4:
-                s2(i - 1)
-                if i % 2 == 0:
-                    vt(i // 2 - 1)
-                    gucopy(i // 2 - 1)
+            if i in (2, 4):
+                s2(i // 2 - 1)
+                vt(i // 2 - 1)
+                gucopy(i // 2 - 1)
                 if i == 4:
                     qu()
             if i >= 1 and state["qz"] < NQ:

@@ -341,8 +341,6 @@ def tile_decode_atten_kernel(tc, x, attentions, out):
                     tr(2 * i + h)
                 for pr in halves[h]:
                     mm(pr)
-                if state["mm"] < 2 * NQ or halves[h]:
-                    dummy(1)
             for h in range(2):
                 if i < NQ:
                     ev(2 * i + h)

@@ -17,10 +17,12 @@ QT = 4
 NQ = 16
 RING = 8
 GROUPS = ((0, 1, 2, 3), (4, 5, 6, 7), (8, 9, 10, 11), (12, 13, 14, 15))
-OE_V = (29, 31)
-EV_V = (31,)
-N_WARM = 6
+NSPLIT = 4
 FIRST_LOADS = (("a", 0), ("a", 1), ("x", 0), ("a", 2), ("x", 1), ("a", 3), ("x", 2), ("a", 4), ("x", 3), ("a", 5), ("a", 6), ("a", 7))
+X_AT = {"s1": (0, 1, 2, 3), "vt": (1, 3), "qu": (2, 4)}
+MAX_UNITS = 3
+V_UNITS_FROM = 28
+V_EV = (29, 31)
 
 
 def tile_decode_atten_kernel(tc, x, attentions, out):
@@ -48,6 +50,10 @@ def tile_decode_atten_kernel(tc, x, attentions, out):
         o1 = {}
         o1sb = {}
         g2 = {}
+        cnts = {}
+        nzs = {}
+        rnzs = {}
+        state = {"load": RING, "st": 0, "unit": 0}
 
         def load_att(q):
             att_q = attp.tile([P, QT, 512], BF16, name="att")
@@ -69,32 +75,15 @@ def tile_decode_atten_kernel(tc, x, attentions, out):
             else:
                 load_x(idx)
 
-        z_codes = keep.tile([P, 512], U32, name="z_codes", align_bytes=64)
-        z_scales = keep.tile([P, 512], U8, name="z_scales", align_bytes=64)
-        z_in = keep.tile([P, 2048], BF16, name="z_in", align_bytes=64)
-        nc.vector.memset(z_in[:], 0.0)
-        nc.vector.quantize_mx(out=z_codes[:].bitcast(FP8X4), scales=z_scales[:], in_=z_in[:])
-        warm = psum.tile([P, 512], F32, name="warm", bufs=1)
-
-        def dummy(n):
-            for k in range(n):
-                nc.tensor.matmul_mx(
-                    out=warm[:],
-                    lhsT=z_codes[:, 0:P].bitcast(FP8X4),
-                    lhsT_scale=z_scales[:, 0:P],
-                    rhs=z_codes[:].bitcast(FP8X4),
-                    rhs_scale=z_scales[:],
-                    start=True,
-                    stop=True,
-                )
-
-        dummy(N_WARM)
-
         ident = keep.tile([P, P], F32, name="ident")
         make_identity(nc, ident[:])
         pool4 = keep.tile([P, 32], F32, name="pool4")
         nc.vector.tensor_reduce(
             out=pool4[:], in_=ident[:].rearrange("k (n d) -> k n d", d=4), axis=AX.X, op=ALU.add
+        )
+        perm = keep.tile([P, P], F32, name="perm")
+        nc.vector.tensor_copy(
+            out=perm[:].rearrange("k (y x) -> k y x", x=8), in_=ident[:].rearrange("k (x y) -> k y x", y=16)
         )
         pool16 = keep.tile([P, 32], BF16, name="pool16")
         nc.vector.tensor_scalar(out=pool16[:], in0=pool4[:], scalar1=1.0 / 16.0, scalar2=None, op0=ALU.mult)
@@ -111,10 +100,6 @@ def tile_decode_atten_kernel(tc, x, attentions, out):
                 nc.vector.tensor_copy(out=dst, in_=src)
             else:
                 nc.scalar.copy(out=dst, in_=src)
-
-        cnts = {}
-        nzs = {}
-        rnzs = {}
 
         def cnt(q, lo=0, hi=QT):
             c_new = small.tile([P, QT], F32, name="cnt")
@@ -159,7 +144,7 @@ def tile_decode_atten_kernel(tc, x, attentions, out):
 
         def tr(pr):
             q, h = pr // 2, pr % 2
-            p_new = psum.tile([P, 2, 2, P], F32, name="p_t", bufs=3)
+            p_new = psum.tile([P, 2, 2, P], F32, name="p_t")
             p_t[pr] = p_new
             for i2 in range(2):
                 words = a_sb[q][:, 2 * h + i2, :].bitcast(F32)
@@ -176,7 +161,7 @@ def tile_decode_atten_kernel(tc, x, attentions, out):
                 g_new = work.tile([P, QT * 512], BF16, name="grouped", align_bytes=64)
                 grouped[q] = g_new
             copy_on(
-                "V" if pr in EV_V else "S",
+                "V" if pr in V_EV else "S",
                 grouped[q][:, h * 1024 : (h + 1) * 1024].bitcast(F32).rearrange("p (i m u) -> p i m u", i=2, u=2),
                 p_t[pr][:].rearrange("p i u m -> p i m u"),
             )
@@ -187,39 +172,48 @@ def tile_decode_atten_kernel(tc, x, attentions, out):
                 out=a_codes[:, cols].bitcast(FP8X4), scales=a_scales[:, cols], in_=grouped[q][:]
             )
 
-        def mm(pr):
-            acc_new = psum.tile([P, 512], F32, name="acc")
-            acc[pr] = acc_new
-            for i2 in range(2):
-                s = 2 * pr + i2
-                nc.tensor.matmul_mx(
-                    out=acc_new[:, i2 * 256 : (i2 + 1) * 256],
-                    lhsT=a_codes[:, s * P : (s + 1) * P].bitcast(FP8X4),
-                    lhsT_scale=a_scales[:, s * P : (s + 1) * P],
-                    rhs=u_codes[:].bitcast(FP8X4),
-                    rhs_scale=u_scales[:],
-                    start=True,
-                    stop=True,
-                )
-
         def group_of(q):
             for g, members in enumerate(GROUPS):
                 if q in members:
                     return g
             return -1
 
-        def oe(pr, eng):
-            g = group_of(pr // 2)
+        def mm(unit):
+            acc_new = psum.tile([P, 512], F32, name="acc")
+            acc[unit] = acc_new
+            if unit[0] == "F":
+                tiles, n0, n = (2 * unit[1], 2 * unit[1] + 1), 0, 256
+            else:
+                tiles, n0, n = tuple(range(QT * unit[1], QT * unit[1] + QT)), unit[2] * P, P
+            for k, s in enumerate(tiles):
+                nc.tensor.matmul_mx(
+                    out=acc_new[:, k * n : (k + 1) * n],
+                    lhsT=a_codes[:, s * P : (s + 1) * P].bitcast(FP8X4),
+                    lhsT_scale=a_scales[:, s * P : (s + 1) * P],
+                    rhs=u_codes[:, n0 : n0 + n].bitcast(FP8X4),
+                    rhs_scale=u_scales[:, n0 : n0 + n],
+                    start=True,
+                    stop=True,
+                )
+
+        def oe(unit, eng):
+            q = unit[1] // 2 if unit[0] == "F" else unit[1]
+            g = group_of(q)
             width = len(GROUPS[g]) * QT
             if g not in f_out:
                 f_new = outp.tile([P, 32, width, 8], F32, name="f_out")
                 f_out[g] = f_new
-            sl = 2 * pr - GROUPS[g][0] * QT
-            copy_on(
-                eng,
-                f_out[g][:, :, sl : sl + 2, :],
-                acc[pr][:].rearrange("p (i q k) -> p q i k", i=2, k=8),
-            )
+            if unit[0] == "F":
+                sl = 2 * unit[1] - GROUPS[g][0] * QT
+                copy_on(eng, f_out[g][:, :, sl : sl + 2, :], acc[unit][:].rearrange("p (i r k) -> p r i k", i=2, k=8))
+            else:
+                sl = (q - GROUPS[g][0]) * QT
+                b = unit[2]
+                copy_on(
+                    eng,
+                    f_out[g][:, b * 16 : (b + 1) * 16, sl : sl + QT, :],
+                    acc[unit][:].rearrange("p (i r k) -> p r i k", i=QT, k=8),
+                )
 
         def st(g):
             width = len(GROUPS[g]) * QT * 8
@@ -234,52 +228,43 @@ def tile_decode_atten_kernel(tc, x, attentions, out):
                     )
 
         def s1(c):
-            for h in range(2):
-                o_new = psum.tile([P, 512], F32, name="acc")
-                o1[(c, h)] = o_new
-                o_view = o_new[:].rearrange(
-                    "p (jl alo tlo ahi thi k) -> p jl alo tlo ahi thi k", jl=4, alo=2, tlo=2, ahi=2, thi=2
-                )
-                for jl in range(4):
-                    for t in range(4):
-                        jq = 4 * h + jl
-                        nc.tensor.matmul(
-                            out=o_view[:, jl, :, t % 2, :, t // 2, :],
-                            lhsT=xs[c][:, t, jq * P : (jq + 1) * P],
-                            rhs=pool16[:].rearrange("q (ahi alo k) -> q alo ahi k", ahi=2, alo=2),
-                            start=True,
-                            stop=True,
-                        )
-
-        def xe(c):
             b, c2 = c // 2, c % 2
             if c2 == 0:
-                o_sb = keep.tile([P, 2048], F32, name="o1sb%d" % b)
-                o1sb[b] = o_sb
-            for h in range(2):
-                nc.scalar.copy(
-                    out=o1sb[b][:].rearrange("p (r c k) -> p r c k", c=2, k=8)[:, h * 64 : (h + 1) * 64, c2, :],
-                    in_=o1[(c, h)][:].rearrange("p (r k) -> p r k", k=8),
-                )
+                o_new = psum.tile([P, 512], F32, name="acc")
+                o1[b] = o_new
+            o_view = o1[b][:].rearrange(
+                "p (alo wb tlo ahi thi c k) -> p wb tlo thi c alo ahi k", alo=2, wb=2, tlo=2, ahi=2, thi=2, c=2
+            )
+            for t in range(4):
+                for wb in range(2):
+                    for dw in range(4):
+                        nc.tensor.matmul(
+                            out=o_view[:, wb, t % 2, t // 2, c2, :, :, :],
+                            lhsT=xs[c][:, t, wb * 512 + dw : (wb + 1) * 512 : 4],
+                            rhs=pool16[:].rearrange("q (ahi alo k) -> q alo ahi k", ahi=2, alo=2),
+                            start=(dw == 0),
+                            stop=(dw == 3),
+                        )
+
+        def xe(b):
+            o_sb = keep.tile([P, 512], F32, name="o1sb%d" % b)
+            o1sb[b] = o_sb
+            nc.scalar.copy(out=o_sb[:], in_=o1[b][:])
 
         def s2(b):
             g_new = psum.tile([P, 512], F32, name="acc")
             g2[b] = g_new
-            g_view = g_new[:].rearrange("p (m alo jq hi) -> p alo jq m hi", m=16, alo=2, jq=8)
-            for jq in range(8):
-                for alo in range(2):
-                    nc.tensor.matmul(
-                        out=g_view[:, alo, jq, :, :],
-                        lhsT=o1sb[b][:, (2 * jq + alo) * P : (2 * jq + alo + 1) * P],
-                        rhs=pool4[:].rearrange("r (hi m) -> r m hi", hi=2),
-                        start=True,
-                        stop=True,
+            g_view = g_new[:].rearrange("p (m alo wb j) -> p alo wb m j", m=16, alo=2, wb=2)
+            for alo in range(2):
+                for wb in range(2):
+                    nc.tensor.transpose(
+                        out=g_view[:, alo, wb, :, :],
+                        in_=o1sb[b][:, (2 * alo + wb) * P : (2 * alo + wb + 1) * P],
+                        identity=perm[:],
                     )
 
         def vt(b):
-            nc.vector.transpose(
-                out=g3[:, b * 512 : (b + 1) * 512], in_=g2[b][:]
-            )
+            nc.vector.transpose(out=g3[:, b * 512 : (b + 1) * 512], in_=g2[b][:])
 
         def gucopy(b):
             for c2 in range(2):
@@ -295,17 +280,26 @@ def tile_decode_atten_kernel(tc, x, attentions, out):
                     op1=ALU.add,
                 )
 
-        def qu():
-            nc.vector.quantize_mx(out=u_codes[:].bitcast(FP8X4), scales=u_scales[:], in_=gu[:])
+        def qu(b):
+            nc.vector.quantize_mx(
+                out=u_codes[:, b * P : (b + 1) * P].bitcast(FP8X4),
+                scales=u_scales[:, b * P : (b + 1) * P],
+                in_=gu[:, b * 512 : (b + 1) * 512],
+            )
 
-        state = {"qz": 0, "mm": 0, "st": 0, "load": RING}
         done = set()
-        pend_v = []
+        need = {}
+        for g, members in enumerate(GROUPS):
+            units = []
+            for q in members:
+                if q < NSPLIT:
+                    units.extend((("H", q, 0), ("H", q, 1)))
+                else:
+                    units.extend((("F", 2 * q), ("F", 2 * q + 1)))
+            need[g] = units
 
         def flush_stores():
-            while state["st"] < len(GROUPS) and all(
-                (2 * q in done) and (2 * q + 1 in done) for q in GROUPS[state["st"]]
-            ):
+            while state["st"] < len(GROUPS) and all(u in done for u in need[state["st"]]):
                 st(state["st"])
                 state["st"] = state["st"] + 1
 
@@ -324,50 +318,81 @@ def tile_decode_atten_kernel(tc, x, attentions, out):
         scl(1)
         fin1(2)
         fin2(2)
-        for i in range(NQ + 10):
-            for pr in pend_v:
-                oe(pr, "V")
-                done.add(pr)
-            pend_v = []
-            flush_stores()
-            todo = []
-            if i >= 5:
-                while len(todo) < 4 and state["mm"] < 2 * state["qz"]:
-                    todo.append(state["mm"])
-                    state["mm"] = state["mm"] + 1
-            halves = (todo[: len(todo) // 2], todo[len(todo) // 2 :])
-            for h in range(2):
-                if i < NQ:
-                    tr(2 * i + h)
-                for pr in halves[h]:
-                    mm(pr)
-            for h in range(2):
-                if i < NQ:
-                    ev(2 * i + h)
-                for pr in halves[h]:
-                    if pr in OE_V:
-                        pend_v.append(pr)
+
+        wait_u = {0: [], 1: []}
+        ready = []
+        have_u = set()
+        pend_v = []
+        late_ev = []
+        tr(0)
+        tr(1)
+        ev(0)
+        ev(1)
+        i = 0
+        while len(done) < 2 * NQ:
+            if i in X_AT["s1"]:
+                c = X_AT["s1"].index(i)
+                s1(c)
+                if c % 2 == 1:
+                    xe(c // 2)
+                    s2(c // 2)
+            if i + 1 < NQ:
+                tr(2 * i + 2)
+                tr(2 * i + 3)
+                for pr in (2 * i + 2, 2 * i + 3):
+                    if pr in V_EV:
+                        late_ev.append(pr)
                     else:
-                        oe(pr, "S")
-                        done.add(pr)
+                        ev(pr)
+            todo = ready[:MAX_UNITS]
+            ready = ready[MAX_UNITS:]
+            for unit in todo:
+                mm(unit)
+            for unit in todo:
+                if state["unit"] >= V_UNITS_FROM and state["unit"] % 2 == 1:
+                    pend_v.append(unit)
+                else:
+                    oe(unit, "S")
+                    done.add(unit)
+                state["unit"] = state["unit"] + 1
             flush_stores()
             if i + 3 < NQ:
                 cnt(i + 3)
+            if i in X_AT["qu"]:
+                b = X_AT["qu"].index(i)
+                qu(b)
+                have_u.add(b)
+                ready.extend(wait_u[b])
+                wait_u[b] = []
             if i + 2 < NQ:
                 scl(i + 2)
             if i + 3 < NQ:
                 fin1(i + 3)
-            if i < 4:
-                s1(i)
-                xe(i)
-            if i in (2, 4):
-                s2(i // 2 - 1)
-                vt(i // 2 - 1)
-                gucopy(i // 2 - 1)
-                if i == 4:
-                    qu()
-            if i >= 1 and state["qz"] < NQ:
-                qz(state["qz"])
-                state["qz"] = state["qz"] + 1
+            if i < NQ:
+                q = i
+                qz(q)
+                if q < NSPLIT:
+                    for b in range(2):
+                        if b in have_u:
+                            ready.append(("H", q, b))
+                        else:
+                            wait_u[b].append(("H", q, b))
+                elif 1 in have_u:
+                    ready.extend((("F", 2 * q), ("F", 2 * q + 1)))
+                else:
+                    wait_u[1].extend((("F", 2 * q), ("F", 2 * q + 1)))
             if i + 3 < NQ:
                 fin2(i + 3)
+            if i in X_AT["vt"]:
+                b = X_AT["vt"].index(i)
+                vt(b)
+                gucopy(b)
+            for pr in late_ev:
+                ev(pr)
+            late_ev = []
+            for unit in pend_v:
+                oe(unit, "V")
+                done.add(unit)
+            pend_v = []
+            flush_stores()
+            i = i + 1

@@ -23,6 +23,8 @@ X_AT = {"s1": (0, 1, 2, 3), "vt": (1, 3), "qu": (2, 4)}
 MAX_UNITS = 3
 V_UNITS_FROM = 28
 V_EV = (29, 31)
+G_FROM = 3
+G_ROWS = 2
 
 
 def tile_decode_atten_kernel(tc, x, attentions, out):
@@ -131,13 +133,23 @@ def tile_decode_atten_kernel(tc, x, attentions, out):
                 a_new = work.tile([P, QT, 512], BF16, name="a_sb")
                 a_sb[q] = a_new
             for i in range(lo, hi):
-                nc.vector.tensor_scalar(
-                    out=a_sb[q][:, i, :],
-                    in0=att[q][:, i, :],
-                    scalar1=rnzs[(q, lo)][:, i : i + 1],
-                    scalar2=None,
-                    op0=ALU.mult,
-                )
+                if q >= G_FROM and i >= QT - G_ROWS:
+                    nc.gpsimd.tensor_scalar(
+                        out=a_sb[q][:, i, :],
+                        in0=att[q][:, i, :],
+                        scalar1=rnzs[(q, lo)][:, i : i + 1],
+                        scalar2=0.0,
+                        op0=ALU.mult,
+                        op1=ALU.add,
+                    )
+                else:
+                    nc.vector.tensor_scalar(
+                        out=a_sb[q][:, i, :],
+                        in0=att[q][:, i, :],
+                        scalar1=rnzs[(q, lo)][:, i : i + 1],
+                        scalar2=None,
+                        op0=ALU.mult,
+                    )
             if hi == QT and state["load"] < NQ:
                 load_att(state["load"])
                 state["load"] = state["load"] + 1

@@ -21,6 +21,7 @@ NSPLIT = 4
 FIRST_LOADS = (("a", 0), ("a", 1), ("x", 0), ("a", 2), ("x", 1), ("a", 3), ("x", 2), ("a", 4), ("x", 3), ("a", 5), ("a", 6), ("a", 7))
 X_AT = {"s1": (0, 1, 2, 3), "vt": (1, 3), "qu": (2, 4)}
 MAX_UNITS = 3
+MX_BANKS = 5
 V_UNITS_FROM = 28
 V_EV = (29, 31)
 G_FROM = 3
@@ -76,6 +77,25 @@ def tile_decode_atten_kernel(tc, x, attentions, out):
                 load_att(idx)
             else:
                 load_x(idx)
+
+        z_codes = keep.tile([P, 512], U32, name="z_codes", align_bytes=64)
+        z_scales = keep.tile([P, 512], U8, name="z_scales", align_bytes=64)
+        z_in = keep.tile([P, 2048], BF16, name="z_in", align_bytes=64)
+        nc.vector.memset(z_in[:], 0.0)
+        nc.vector.quantize_mx(out=z_codes[:].bitcast(FP8X4), scales=z_scales[:], in_=z_in[:])
+        warm = psum.tile([P, 512], F32, name="warm", bufs=1)
+
+        def dummy(n):
+            for k in range(n):
+                nc.tensor.matmul_mx(
+                    out=warm[:],
+                    lhsT=z_codes[:, 0:P].bitcast(FP8X4),
+                    lhsT_scale=z_scales[:, 0:P],
+                    rhs=z_codes[:].bitcast(FP8X4),
+                    rhs_scale=z_scales[:],
+                    start=True,
+                    stop=True,
+                )
 
         ident = keep.tile([P, P], F32, name="ident")
         make_identity(nc, ident[:])
@@ -156,7 +176,7 @@ def tile_decode_atten_kernel(tc, x, attentions, out):
 
         def tr(pr):
             q, h = pr // 2, pr % 2
-            p_new = psum.tile([P, 2, 2, P], F32, name="p_t")
+            p_new = psum.tile([P, 2, 2, P], F32, name="p_t", bufs=3)
             p_t[pr] = p_new
             for i2 in range(2):
                 words = a_sb[q][:, 2 * h + i2, :].bitcast(F32)
@@ -358,6 +378,8 @@ def tile_decode_atten_kernel(tc, x, attentions, out):
                         ev(pr)
             todo = ready[:MAX_UNITS]
             ready = ready[MAX_UNITS:]
+            if i + 1 < NQ:
+                dummy(MX_BANKS - len(todo))
             for unit in todo:
                 mm(unit)
             for unit in todo:

@@ -22,6 +22,7 @@ FIRST_LOADS = (("a", 0), ("a", 1), ("x", 0), ("a", 2), ("x", 1), ("a", 3), ("x",
 X_AT = {"s1": (0, 1, 2, 3), "vt": (1, 3), "qu": (2, 4)}
 MAX_UNITS = 3
 MX_BANKS = 5
+MX_BANKS_X = 2
 V_UNITS_FROM = 28
 V_EV = (29, 31)
 G_FROM = 3
@@ -379,7 +380,7 @@ def tile_decode_atten_kernel(tc, x, attentions, out):
             todo = ready[:MAX_UNITS]
             ready = ready[MAX_UNITS:]
             if i + 1 < NQ:
-                dummy(MX_BANKS - len(todo))
+                dummy((MX_BANKS_X if i in X_AT["s1"] else MX_BANKS) - len(todo))
             for unit in todo:
                 mm(unit)
             for unit in todo:

@@ -17,15 +17,15 @@ QT = 4
 NQ = 16
 RING = 8
 GROUPS = ((0, 1, 2, 3), (4, 5, 6, 7), (8, 9, 10, 11), (12, 13, 14, 15))
-NSPLIT = 4
-FIRST_LOADS = (("a", 0), ("a", 1), ("x", 0), ("a", 2), ("x", 1), ("a", 3), ("x", 2), ("a", 4), ("x", 3), ("a", 5), ("a", 6), ("a", 7))
-X_AT = {"s1": (0, 1, 2, 3), "vt": (1, 3), "qu": (2, 4)}
+NSPLIT = 5
+FIRST_LOADS = (("a", 0), ("a", 1), ("a", 2), ("a", 3), ("x", 0), ("a", 4), ("x", 1), ("a", 5), ("x", 2), ("a", 6), ("x", 3), ("a", 7))
+X_AT = {"s1": (1, 2, 3, 4), "vt": (2, 4), "qu": (3, 5)}
 MAX_UNITS = 3
 MX_BANKS = 5
 MX_BANKS_X = 2
 V_UNITS_FROM = 28
 V_EV = (29, 31)
-G_FROM = 3
+G_FROM = 2
 G_ROWS = 2
 
 

from contextlib import ExitStack

import concourse.mybir as mybir
from concourse.masks import make_identity

FLOPS = 2 * 8192 * 512 * 256

BF16 = mybir.dt.bfloat16
F32 = mybir.dt.float32
U32 = mybir.dt.uint32
U8 = mybir.dt.uint8
FP8X4 = mybir.dt.float8_e4m3fn_x4
ALU = mybir.AluOpType
AX = mybir.AxisListType
P = 128
QT = 4
NQ = 16
RING = 8
GROUPS = ((0, 1, 2, 3), (4, 5, 6, 7), (8, 9, 10, 11), (12, 13, 14, 15))
NSPLIT = 5
FIRST_LOADS = (("a", 0), ("a", 1), ("a", 2), ("a", 3), ("x", 0), ("a", 4), ("x", 1), ("a", 5), ("x", 2), ("a", 6), ("x", 3), ("a", 7))
X_AT = {"s1": (1, 2, 3, 4), "vt": (2, 4), "qu": (3, 5)}
MAX_UNITS = 3
MX_BANKS = 5
MX_BANKS_X = 2
V_UNITS_FROM = 28
V_EV = (29, 31)
G_FROM = 2
G_ROWS = 2


def tile_decode_atten_kernel(tc, x, attentions, out):
    nc = tc.nc
    xv = x[0].rearrange("c (t q) w -> q c t w", q=P)
    av = attentions[0, 0].rearrange("(m s) j -> m s j", s=64)
    ov = out[0].rearrange("c (lh kh) w -> c lh kh w", kh=8)

    with ExitStack() as ctx:
        keep = ctx.enter_context(tc.tile_pool(name="keep", bufs=1))
        attp = ctx.enter_context(tc.tile_pool(name="attp", bufs=RING))
        small = ctx.enter_context(tc.tile_pool(name="small", bufs=4))
        work = ctx.enter_context(tc.tile_pool(name="work", bufs=4))
        outp = ctx.enter_context(tc.tile_pool(name="outp", bufs=3))
        psum = ctx.enter_context(tc.psum_pool(name="psum", bufs=4))
        ctx.enter_context(tc.manual_schedule())

        att = {}
        xs = {}
        a_sb = {}
        grouped = {}
        p_t = {}
        acc = {}
        f_out = {}
        o1 = {}
        o1sb = {}
        g2 = {}
        cnts = {}
        nzs = {}
        rnzs = {}
        state = {"load": RING, "st": 0, "unit": 0}

        def load_att(q):
            att_q = attp.tile([P, QT, 512], BF16, name="att")
            att[q] = att_q
            if q == 0:
                for h in range(2):
                    nc.sync.dma_start(out=att_q[:, 2 * h : 2 * h + 2, :], in_=av[:, 2 * h : 2 * h + 2, :])
            else:
                nc.sync.dma_start(out=att_q[:], in_=av[:, q * QT : (q + 1) * QT, :])

        def load_x(c):
            xs_c = keep.tile([P, 4, 1024], BF16, name="xs%d" % c)
            xs[c] = xs_c
            nc.sync.dma_start(out=xs_c[:], in_=xv[:, c, :, :])

        for kind, idx in FIRST_LOADS:
            if kind == "a":
                load_att(idx)
            else:
                load_x(idx)

        z_codes = keep.tile([P, 512], U32, name="z_codes", align_bytes=64)
        z_scales = keep.tile([P, 512], U8, name="z_scales", align_bytes=64)
        z_in = keep.tile([P, 2048], BF16, name="z_in", align_bytes=64)
        nc.vector.memset(z_in[:], 0.0)
        nc.vector.quantize_mx(out=z_codes[:].bitcast(FP8X4), scales=z_scales[:], in_=z_in[:])
        warm = psum.tile([P, 512], F32, name="warm", bufs=1)

        def dummy(n):
            for k in range(n):
                nc.tensor.matmul_mx(
                    out=warm[:],
                    lhsT=z_codes[:, 0:P].bitcast(FP8X4),
                    lhsT_scale=z_scales[:, 0:P],
                    rhs=z_codes[:].bitcast(FP8X4),
                    rhs_scale=z_scales[:],
                    start=True,
                    stop=True,
                )

        ident = keep.tile([P, P], F32, name="ident")
        make_identity(nc, ident[:])
        pool4 = keep.tile([P, 32], F32, name="pool4")
        nc.vector.tensor_reduce(
            out=pool4[:], in_=ident[:].rearrange("k (n d) -> k n d", d=4), axis=AX.X, op=ALU.add
        )
        perm = keep.tile([P, P], F32, name="perm")
        nc.vector.tensor_copy(
            out=perm[:].rearrange("k (y x) -> k y x", x=8), in_=ident[:].rearrange("k (x y) -> k y x", y=16)
        )
        pool16 = keep.tile([P, 32], BF16, name="pool16")
        nc.vector.tensor_scalar(out=pool16[:], in0=pool4[:], scalar1=1.0 / 16.0, scalar2=None, op0=ALU.mult)

        a_codes = keep.tile([P, 8192], U32, name="a_codes", align_bytes=64)
        a_scales = keep.tile([P, 8192], U8, name="a_scales", align_bytes=64)
        u_codes = keep.tile([P, 256], U32, name="u_codes", align_bytes=64)
        u_scales = keep.tile([P, 256], U8, name="u_scales", align_bytes=64)
        g3 = keep.tile([P, 1024], F32, name="g3", align_bytes=64)
        gu = keep.tile([P, 1024], BF16, name="gu", align_bytes=64)

        def copy_on(eng, dst, src):
            if eng == "V":
                nc.vector.tensor_copy(out=dst, in_=src)
            else:
                nc.scalar.copy(out=dst, in_=src)

        def cnt(q, lo=0, hi=QT):
            c_new = small.tile([P, QT], F32, name="cnt")
            cnts[(q, lo)] = c_new
            for i in range(lo, hi):
                junk = small.tile([P, 512], BF16, name="junk")
                nc.vector.tensor_scalar(
                    out=junk[:],
                    in0=att[q][:, i, :],
                    scalar1=0.0,
                    scalar2=None,
                    op0=ALU.not_equal,
                    op1=ALU.add,
                    accum_out=c_new[:, i : i + 1],
                )

        def fin1(q, lo=0, hi=QT):
            nz = small.tile([P, QT], F32, name="nz")
            nzs[(q, lo)] = nz
            nc.vector.tensor_scalar_add(out=nz[:, lo:hi], in0=cnts[(q, lo)][:, lo:hi], scalar1=1e-05)

        def fin2(q, lo=0, hi=QT):
            rnz = small.tile([P, QT], F32, name="rnz")
            rnzs[(q, lo)] = rnz
            nc.vector.reciprocal(out=rnz[:, lo:hi], in_=nzs[(q, lo)][:, lo:hi])

        def scl(q, lo=0, hi=QT):
            if lo == 0:
                a_new = work.tile([P, QT, 512], BF16, name="a_sb")
                a_sb[q] = a_new
            for i in range(lo, hi):
                if q >= G_FROM and i >= QT - G_ROWS:
                    nc.gpsimd.tensor_scalar(
                        out=a_sb[q][:, i, :],
                        in0=att[q][:, i, :],
                        scalar1=rnzs[(q, lo)][:, i : i + 1],
                        scalar2=0.0,
                        op0=ALU.mult,
                        op1=ALU.add,
                    )
                else:
                    nc.vector.tensor_scalar(
                        out=a_sb[q][:, i, :],
                        in0=att[q][:, i, :],
                        scalar1=rnzs[(q, lo)][:, i : i + 1],
                        scalar2=None,
                        op0=ALU.mult,
                    )
            if hi == QT and state["load"] < NQ:
                load_att(state["load"])
                state["load"] = state["load"] + 1

        def tr(pr):
            q, h = pr // 2, pr % 2
            p_new = psum.tile([P, 2, 2, P], F32, name="p_t", bufs=3)
            p_t[pr] = p_new
            for i2 in range(2):
                words = a_sb[q][:, 2 * h + i2, :].bitcast(F32)
                for u in range(2):
                    nc.tensor.transpose(
                        out=p_new[:, i2, u, :],
                        in_=words[:, u * P : (u + 1) * P],
                        identity=ident[:],
                    )

        def ev(pr):
            q, h = pr // 2, pr % 2
            if h == 0:
                g_new = work.tile([P, QT * 512], BF16, name="grouped", align_bytes=64)
                grouped[q] = g_new
            copy_on(
                "V" if pr in V_EV else "S",
                grouped[q][:, h * 1024 : (h + 1) * 1024].bitcast(F32).rearrange("p (i m u) -> p i m u", i=2, u=2),
                p_t[pr][:].rearrange("p i u m -> p i m u"),
            )

        def qz(q):
            cols = slice(q * 512, (q + 1) * 512)
            nc.vector.quantize_mx(
                out=a_codes[:, cols].bitcast(FP8X4), scales=a_scales[:, cols], in_=grouped[q][:]
            )

        def group_of(q):
            for g, members in enumerate(GROUPS):
                if q in members:
                    return g
            return -1

        def mm(unit):
            acc_new = psum.tile([P, 512], F32, name="acc")
            acc[unit] = acc_new
            if unit[0] == "F":
                tiles, n0, n = (2 * unit[1], 2 * unit[1] + 1), 0, 256
            else:
                tiles, n0, n = tuple(range(QT * unit[1], QT * unit[1] + QT)), unit[2] * P, P
            for k, s in enumerate(tiles):
                nc.tensor.matmul_mx(
                    out=acc_new[:, k * n : (k + 1) * n],
                    lhsT=a_codes[:, s * P : (s + 1) * P].bitcast(FP8X4),
                    lhsT_scale=a_scales[:, s * P : (s + 1) * P],
                    rhs=u_codes[:, n0 : n0 + n].bitcast(FP8X4),
                    rhs_scale=u_scales[:, n0 : n0 + n],
                    start=True,
                    stop=True,
                )

        def oe(unit, eng):
            q = unit[1] // 2 if unit[0] == "F" else unit[1]
            g = group_of(q)
            width = len(GROUPS[g]) * QT
            if g not in f_out:
                f_new = outp.tile([P, 32, width, 8], F32, name="f_out")
                f_out[g] = f_new
            if unit[0] == "F":
                sl = 2 * unit[1] - GROUPS[g][0] * QT
                copy_on(eng, f_out[g][:, :, sl : sl + 2, :], acc[unit][:].rearrange("p (i r k) -> p r i k", i=2, k=8))
            else:
                sl = (q - GROUPS[g][0]) * QT
                b = unit[2]
                copy_on(
                    eng,
                    f_out[g][:, b * 16 : (b + 1) * 16, sl : sl + QT, :],
                    acc[unit][:].rearrange("p (i r k) -> p r i k", i=QT, k=8),
                )

        def st(g):
            width = len(GROUPS[g]) * QT * 8
            last = g == len(GROUPS) - 1
            for c in range(4):
                for hf in range(2):
                    w0 = hf * 512 + GROUPS[g][0] * QT * 8
                    queue = nc.scalar if (last and hf == 1) else nc.sync
                    queue.dma_start(
                        out=ov[c, :, :, w0 : w0 + width],
                        in_=f_out[g][hf:P:2, c * 8 : (c + 1) * 8, :, :].rearrange("m kh s kw -> m kh (s kw)"),
                    )

        def s1(c):
            b, c2 = c // 2, c % 2
            if c2 == 0:
                o_new = psum.tile([P, 512], F32, name="acc")
                o1[b] = o_new
            o_view = o1[b][:].rearrange(
                "p (alo wb tlo ahi thi c k) -> p wb tlo thi c alo ahi k", alo=2, wb=2, tlo=2, ahi=2, thi=2, c=2
            )
            for t in range(4):
                for wb in range(2):
                    for dw in range(4):
                        nc.tensor.matmul(
                            out=o_view[:, wb, t % 2, t // 2, c2, :, :, :],
                            lhsT=xs[c][:, t, wb * 512 + dw : (wb + 1) * 512 : 4],
                            rhs=pool16[:].rearrange("q (ahi alo k) -> q alo ahi k", ahi=2, alo=2),
                            start=(dw == 0),
                            stop=(dw == 3),
                        )

        def xe(b):
            o_sb = keep.tile([P, 512], F32, name="o1sb%d" % b)
            o1sb[b] = o_sb
            nc.scalar.copy(out=o_sb[:], in_=o1[b][:])

        def s2(b):
            g_new = psum.tile([P, 512], F32, name="acc")
            g2[b] = g_new
            g_view = g_new[:].rearrange("p (m alo wb j) -> p alo wb m j", m=16, alo=2, wb=2)
            for alo in range(2):
                for wb in range(2):
                    nc.tensor.transpose(
                        out=g_view[:, alo, wb, :, :],
                        in_=o1sb[b][:, (2 * alo + wb) * P : (2 * alo + wb + 1) * P],
                        identity=perm[:],
                    )

        def vt(b):
            nc.vector.transpose(out=g3[:, b * 512 : (b + 1) * 512], in_=g2[b][:])

        def gucopy(b):
            for c2 in range(2):
                c = 2 * b + c2
                nc.gpsimd.tensor_scalar(
                    out=gu[:, c * 256 : (c + 1) * 256].rearrange("p (kh m lo) -> p kh m lo", kh=8, m=16),
                    in0=g3[:, b * 512 : (b + 1) * 512].rearrange("p (lo m c kh) -> p c kh m lo", lo=2, m=16, c=2)[
                        :, c2, :, :, :
                    ],
                    scalar1=1.0,
                    scalar2=0.0,
                    op0=ALU.mult,
                    op1=ALU.add,
                )

        def qu(b):
            nc.vector.quantize_mx(
                out=u_codes[:, b * P : (b + 1) * P].bitcast(FP8X4),
                scales=u_scales[:, b * P : (b + 1) * P],
                in_=gu[:, b * 512 : (b + 1) * 512],
            )

        done = set()
        need = {}
        for g, members in enumerate(GROUPS):
            units = []
            for q in members:
                if q < NSPLIT:
                    units.extend((("H", q, 0), ("H", q, 1)))
                else:
                    units.extend((("F", 2 * q), ("F", 2 * q + 1)))
            need[g] = units

        def flush_stores():
            while state["st"] < len(GROUPS) and all(u in done for u in need[state["st"]]):
                st(state["st"])
                state["st"] = state["st"] + 1

        cnt(0, 0, 2)
        fin1(0, 0, 2)
        fin2(0, 0, 2)
        scl(0, 0, 2)
        cnt(0, 2, 4)
        fin1(0, 2, 4)
        cnt(1)
        fin2(0, 2, 4)
        scl(0, 2, 4)
        fin1(1)
        cnt(2)
        fin2(1)
        scl(1)
        fin1(2)
        fin2(2)

        wait_u = {0: [], 1: []}
        ready = []
        have_u = set()
        pend_v = []
        late_ev = []
        tr(0)
        tr(1)
        ev(0)
        ev(1)
        i = 0
        while len(done) < 2 * NQ:
            if i in X_AT["s1"]:
                c = X_AT["s1"].index(i)
                s1(c)
                if c % 2 == 1:
                    xe(c // 2)
                    s2(c // 2)
            if i + 1 < NQ:
                tr(2 * i + 2)
                tr(2 * i + 3)
                for pr in (2 * i + 2, 2 * i + 3):
                    if pr in V_EV:
                        late_ev.append(pr)
                    else:
                        ev(pr)
            todo = ready[:MAX_UNITS]
            ready = ready[MAX_UNITS:]
            if i + 1 < NQ:
                dummy((MX_BANKS_X if i in X_AT["s1"] else MX_BANKS) - len(todo))
            for unit in todo:
                mm(unit)
            for unit in todo:
                if state["unit"] >= V_UNITS_FROM and state["unit"] % 2 == 1:
                    pend_v.append(unit)
                else:
                    oe(unit, "S")
                    done.add(unit)
                state["unit"] = state["unit"] + 1
            flush_stores()
            if i + 3 < NQ:
                cnt(i + 3)
            if i in X_AT["qu"]:
                b = X_AT["qu"].index(i)
                qu(b)
                have_u.add(b)
                ready.extend(wait_u[b])
                wait_u[b] = []
            if i + 2 < NQ:
                scl(i + 2)
            if i + 3 < NQ:
                fin1(i + 3)
            if i < NQ:
                q = i
                qz(q)
                if q < NSPLIT:
                    for b in range(2):
                        if b in have_u:
                            ready.append(("H", q, b))
                        else:
                            wait_u[b].append(("H", q, b))
                elif 1 in have_u:
                    ready.extend((("F", 2 * q), ("F", 2 * q + 1)))
                else:
                    wait_u[1].extend((("F", 2 * q), ("F", 2 * q + 1)))
            if i + 3 < NQ:
                fin2(i + 3)
            if i in X_AT["vt"]:
                b = X_AT["vt"].index(i)
                vt(b)
                gucopy(b)
            for pr in late_ev:
                ev(pr)
            late_ev = []
            for unit in pend_v:
                oe(unit, "V")
                done.add(unit)
            pend_v = []
            flush_stores()
            i = i + 1
